import numpy as np
import ml_dtypes


def mxq(x, axis, fmt="e4m3"):
    dtype, down = {"e4m3": (ml_dtypes.float8_e4m3fn, 7), "e5m2": (ml_dtypes.float8_e5m2, 14)}[fmt]
    v = np.moveaxis(np.asarray(x, np.float32).astype(ml_dtypes.bfloat16).astype(np.float64), axis, -1)
    blocks = v.reshape(v.shape[:-1] + (-1, 32))
    amax = np.abs(blocks).max(-1, keepdims=True)
    byte = np.maximum(np.where(amax > 0, np.frexp(amax)[1] - 1 + 127, 0) - down, 1)
    scale = np.exp2(byte - 127.0)
    codes = (blocks / scale).astype(np.float32).astype(dtype).astype(np.float64)
    return np.moveaxis((codes * scale).reshape(v.shape), -1, axis)


WIDE = False


def mx_kscale(k):
    if not WIDE:
        return np.ones(k)
    levels = np.array([10, -10, 5, -5, 0])
    if k % 512:
        return np.exp2(np.random.permutation(np.resize(levels, k // 32))).repeat(32)
    a = np.empty((k // 512, 16))
    for p in range(k // 512):
        a[p, :8] = np.random.permutation(np.resize(levels, 8))
        for g in range(8):
            far = levels[np.abs(levels - a[p, g]) >= 10]
            a[p, g + 8] = far[np.random.randint(len(far))]
    return np.exp2(a.ravel()).repeat(32)


BF16 = ml_dtypes.bfloat16


def bf(x):
    return np.asarray(x, np.float32).astype(BF16)


def f64(x):
    return np.asarray(x).astype(np.float64)


B, C, HH, WW = 1, 512, 32, 32
N = HH * WW


def setup_inputs():
    s, t = mx_kscale(C), mx_kscale(C)
    return {"x": bf(np.random.standard_normal((B, C, HH, WW)) * s[None, :, None, None]),
            "Wq": bf(np.random.standard_normal((C, C)) * 1.4 / np.sqrt(C) * t[:, None] / s[None, :]),
            "bq": bf(np.random.standard_normal(C) * 0.2 * t),
            "k": bf(np.random.standard_normal((B, N, C)) * 1.4 / t)}


def reference(x, Wq, bq, k):
    xt = f64(x).reshape(B, C, N)
    q = (mxq(xt, 1, "e4m3").transpose(0, 2, 1) @ mxq(f64(Wq), 1, "e4m3").T) + f64(bq)
    scores = mxq(q / np.sqrt(C), 2, "e4m3") @ mxq(f64(k), 2, "e4m3").transpose(0, 2, 1)
    e = np.exp(scores - scores.max(-1, keepdims=True))
    return e / e.sum(-1, keepdims=True)

@@ -1,0 +1,250 @@
+import math
+from contextlib import ExitStack
+
+import concourse.masks as masks
+import concourse.mybir as mybir
+
+F32 = mybir.dt.float32
+BF16 = mybir.dt.bfloat16
+U32 = mybir.dt.uint32
+U8 = mybir.dt.uint8
+FP8X4 = mybir.dt.float8_e4m3fn_x4
+ACT = mybir.ActivationFunctionType
+ALU = mybir.AluOpType
+AXIS = mybir.AxisListType
+
+P = 128
+PACK = 4
+CHANNELS = P * PACK
+TOKENS = 1024
+HALF = 512
+HALVES = TOKENS // HALF
+WORD_PAIR = 2
+INV_SQRT_CHANNELS = 1.0 / math.sqrt(CHANNELS)
+TILES = TOKENS // P
+SCORE_LEAD = 2
+LAG = 2
+
+FLOPS = 2 * TOKENS * CHANNELS * CHANNELS + 2 * TOKENS * TOKENS * CHANNELS
+
+
+def quantise(nc, pool, grouped, label):
+    codes = pool.tile([P, HALF], U32, name="%s_codes" % label, align_bytes=64)
+    scales = pool.tile([P, HALF], U8, name="%s_scales" % label, align_bytes=64)
+    nc.vector.quantize_mx(out=codes[:].bitcast(FP8X4), scales=scales[:], in_=grouped[:])
+    return codes, scales
+
+
+def interleave_planes(nc, pool, planes, label):
+    grouped = pool.tile([P, HALF * PACK], BF16, name="%s_grouped" % label, align_bytes=64)
+    nc.vector.tensor_copy(
+        out=grouped[:].rearrange("p (c i t) -> p c t i", i=4, t=PACK),
+        in_=planes[:].rearrange("p t (c i) -> p c t i", i=4),
+    )
+    return grouped
+
+
+def channels_to_partitions(nc, pool, psum, identity, rows, label):
+    row_words = rows[:].bitcast(F32).rearrange("p (a w u) -> p a u w", a=PACK, u=WORD_PAIR)
+    grouped = pool.tile([P, HALF * PACK], BF16, name="%s_grouped" % label, align_bytes=64)
+    grouped_words = grouped[:].bitcast(F32).rearrange("p (a r u) -> p a r u", a=PACK, u=WORD_PAIR)
+    tiles_per_bank = 2
+    for first in range(0, PACK, tiles_per_bank):
+        bank = psum.tile([P, HALF], F32, tag="bank")
+        flipped = bank[:].rearrange("p (a u r) -> p a u r", a=tiles_per_bank, u=WORD_PAIR)
+        for a in range(tiles_per_bank):
+            for u in range(WORD_PAIR):
+                nc.tensor.transpose(flipped[:, a, u, :], row_words[:, first + a, u, :], identity[:])
+        nc.scalar.copy(
+            out=grouped_words[:, first : first + tiles_per_bank],
+            in_=flipped.rearrange("p a u r -> p a r u"),
+        )
+    return grouped
+
+
+def tile_visionattention_pa_kernel(tc, x, Wq, bq, k, out):
+    nc = tc.nc
+    x_rows_dram = x.rearrange("b c h w -> (b c) (h w)")
+    k_rows_dram = k.flatten_outer_dims()
+    out_rows_dram = out.flatten_outer_dims()
+
+    with ExitStack() as ctx:
+        keep = ctx.enter_context(tc.tile_pool(name="keep", bufs=1))
+        rows_pool = ctx.enter_context(tc.tile_pool(name="rows", bufs=LAG + 3))
+        psum = ctx.enter_context(tc.psum_pool(name="psum", bufs=8))
+
+        wq_rows = keep.tile([P, PACK * CHANNELS], BF16)
+        nc.sync.dma_start(out=wq_rows[:], in_=Wq.rearrange("(r t) c -> r (t c)", t=PACK))
+        x_planes = []
+        k_rows = []
+        for h in range(HALVES):
+            cols = slice(h * HALF, (h + 1) * HALF)
+            x_half = keep.tile([P, PACK, HALF], BF16, name="x_planes%d" % h)
+            nc.sync.dma_start(
+                out=x_half[:], in_=x_rows_dram[:, cols].rearrange("(p t) n -> p t n", t=PACK)
+            )
+            x_planes.append(x_half)
+            k_half = keep.tile([P, PACK * CHANNELS], BF16, name="k_rows%d" % h)
+            nc.sync.dma_start(out=k_half[:], in_=k_rows_dram[cols, :].rearrange("(r a) c -> r (a c)", a=PACK))
+            k_rows.append(k_half)
+        bq_raw = keep.tile([P, PACK], BF16)
+        nc.scalar.dma_start(out=bq_raw[:], in_=bq.rearrange("(r t) -> r t", t=PACK))
+
+        identity = keep.tile([P, P], F32)
+        masks.make_identity(nc, identity[:])
+        warm = keep.tile([P, 1], F32)
+        nc.vector.memset(warm[:], 0.0)
+        nc.scalar.activation(out=warm[:], in_=warm[:], func=ACT.Exp)
+        bias = keep.tile([P, PACK], F32)
+        nc.vector.tensor_scalar_mul(out=bias[:], in0=bq_raw[:], scalar1=INV_SQRT_CHANNELS)
+
+        wq_grouped = channels_to_partitions(nc, keep, psum, identity, wq_rows, "wq")
+        wq_codes, wq_scales = quantise(nc, keep, wq_grouped, "wq")
+
+        x_mx = []
+        k_mx = []
+        for h in range(HALVES):
+            x_grouped = interleave_planes(nc, keep, x_planes[h], "x%d" % h)
+            x_mx.append(quantise(nc, keep, x_grouped, "x%d" % h))
+            k_grouped = channels_to_partitions(nc, keep, psum, identity, k_rows[h], "k%d" % h)
+            k_mx.append(quantise(nc, keep, k_grouped, "k%d" % h))
+
+        q_mx = []
+        for h in range(HALVES):
+            x_codes, x_scales = x_mx[h]
+            q_planes = keep.tile([P, PACK, HALF], BF16, name="q_planes%d" % h)
+            for t in range(PACK):
+                out_channels = slice(t * P, (t + 1) * P)
+                bank = psum.tile([P, HALF], F32, tag="bank")
+                nc.tensor.matmul_mx(
+                    out=bank[:],
+                    lhsT=wq_codes[:, out_channels].bitcast(FP8X4),
+                    lhsT_scale=wq_scales[:, out_channels],
+                    rhs=x_codes[:].bitcast(FP8X4),
+                    rhs_scale=x_scales[:],
+                    start=True,
+                    stop=True,
+                )
+                nc.scalar.activation(
+                    out=q_planes[:, t, :],
+                    in_=bank[:],
+                    func=ACT.Identity,
+                    bias=bias[:, t : t + 1],
+                    scale=INV_SQRT_CHANNELS,
+                )
+            q_grouped = interleave_planes(nc, keep, q_planes, "q%d" % h)
+            q_mx.append(quantise(nc, keep, q_grouped, "q%d" % h))
+
+        scores = {}
+        maxes = {}
+        neg_max = {}
+        probs = {}
+        sums = {}
+        row_sum = {}
+        inv_sum = {}
+
+        def score(g):
+            q_codes, q_scales = q_mx[(g * P) // HALF]
+            tokens = slice((g * P) % HALF, (g * P) % HALF + P)
+            scores[g] = []
+            for h in range(HALVES):
+                k_codes, k_scales = k_mx[h]
+                bank = psum.tile([P, HALF], F32, tag="bank")
+                nc.tensor.matmul_mx(
+                    out=bank[:],
+                    lhsT=q_codes[:, tokens].bitcast(FP8X4),
+                    lhsT_scale=q_scales[:, tokens],
+                    rhs=k_codes[:].bitcast(FP8X4),
+                    rhs_scale=k_scales[:],
+                    start=True,
+                    stop=True,
+                )
+                scores[g].append(bank)
+
+        def bank_maximum(g, h):
+            if h == 0:
+                bank_maxes = rows_pool.tile([P, HALVES], F32, tag="maxes")
+                maxes[g] = bank_maxes
+            nc.vector.tensor_reduce(
+                out=maxes[g][:, h : h + 1], in_=scores[g][h][:], axis=AXIS.X, op=ALU.max
+            )
+
+        def negate_maximum(g):
+            minus = rows_pool.tile([P, 1], F32, tag="neg_max")
+            nc.vector.tensor_scalar(
+                out=minus[:],
+                in0=maxes[g][:, 0:1],
+                scalar1=maxes[g][:, 1:2],
+                scalar2=-1.0,
+                op0=ALU.max,
+                op1=ALU.mult,
+            )
+            neg_max[g] = minus
+
+        def exponentials(g):
+            row_tile = rows_pool.tile([P, TOKENS], F32, tag="probs")
+            bank_sums = rows_pool.tile([P, HALVES], F32, tag="sums")
+            for h in range(HALVES):
+                nc.scalar.activation(
+                    out=row_tile[:, h * HALF : (h + 1) * HALF].rearrange("p (r a) -> p r a", a=PACK),
+                    in_=scores[g][h][:].rearrange("p (a r) -> p r a", a=PACK),
+                    func=ACT.Exp,
+                    bias=neg_max[g][:, 0:1],
+                    scale=1.0,
+                    accum_out=bank_sums[:, h : h + 1],
+                )
+            probs[g] = row_tile
+            sums[g] = bank_sums
+
+        def add_sums(g):
+            total = rows_pool.tile([P, 1], F32, tag="row_sum")
+            nc.vector.tensor_add(out=total[:], in0=sums[g][:, 0:1], in1=sums[g][:, 1:2])
+            row_sum[g] = total
+
+        def invert_sum(g):
+            inverse = rows_pool.tile([P, 1], F32, tag="inv_sum")
+            nc.vector.reciprocal(out=inverse[:], in_=row_sum[g][:])
+            inv_sum[g] = inverse
+
+        def scale_and_store(g):
+            rows = slice(g * P, (g + 1) * P)
+            if g < TILES - LAG:
+                nc.gpsimd.tensor_scalar(
+                    out=probs[g][:],
+                    in0=probs[g][:],
+                    scalar1=inv_sum[g][:, 0:1],
+                    scalar2=0.0,
+                    op0=ALU.mult,
+                    op1=ALU.add,
+                )
+                nc.sync.dma_start(out=out_rows_dram[rows, :], in_=probs[g][:])
+            else:
+                for h in range(HALVES):
+                    cols = slice(h * HALF, (h + 1) * HALF)
+                    nc.vector.tensor_scalar_mul(
+                        out=probs[g][:, cols], in0=probs[g][:, cols], scalar1=inv_sum[g][:, 0:1]
+                    )
+                    nc.sync.dma_start(out=out_rows_dram[rows, cols], in_=probs[g][:, cols])
+
+        def is_tile(g):
+            return 0 <= g < TILES
+
+        with tc.manual_schedule():
+            for g in range(SCORE_LEAD):
+                score(g)
+            for s in range(TILES + LAG):
+                if is_tile(s + SCORE_LEAD):
+                    score(s + SCORE_LEAD)
+                if is_tile(s):
+                    bank_maximum(s, 0)
+                if is_tile(s - LAG):
+                    add_sums(s - LAG)
+                if is_tile(s):
+                    bank_maximum(s, 1)
+                if is_tile(s - LAG):
+                    invert_sum(s - LAG)
+                if is_tile(s):
+                    negate_maximum(s)
+                    exponentials(s)
+                if is_tile(s - LAG):
+                    scale_and_store(s - LAG)

@@ -171,14 +171,7 @@ def tile_visionattention_pa_kernel(tc, x, Wq, bq, k, out):
 
         def negate_maximum(g):
             minus = rows_pool.tile([P, 1], F32, tag="neg_max")
-            nc.vector.tensor_scalar(
-                out=minus[:],
-                in0=maxes[g][:, 0:1],
-                scalar1=maxes[g][:, 1:2],
-                scalar2=-1.0,
-                op0=ALU.max,
-                op1=ALU.mult,
-            )
+            nc.vector.tensor_reduce(out=minus[:], in_=maxes[g][:], axis=AXIS.X, op=ALU.max, negate=True)
             neg_max[g] = minus
 
         def exponentials(g):
@@ -198,7 +191,7 @@ def tile_visionattention_pa_kernel(tc, x, Wq, bq, k, out):
 
         def add_sums(g):
             total = rows_pool.tile([P, 1], F32, tag="row_sum")
-            nc.vector.tensor_add(out=total[:], in0=sums[g][:, 0:1], in1=sums[g][:, 1:2])
+            nc.vector.tensor_reduce(out=total[:], in_=sums[g][:], axis=AXIS.X, op=ALU.add)
             row_sum[g] = total
 
         def invert_sum(g):

@@ -19,47 +19,14 @@ CHANNELS = P * PACK
 TOKENS = 1024
 HALF = 512
 HALVES = TOKENS // HALF
+CHUNK = 256
+CHUNKS = TOKENS // CHUNK
 WORD_PAIR = 2
 INV_SQRT_CHANNELS = 1.0 / math.sqrt(CHANNELS)
 TILES = TOKENS // P
-SCORE_LEAD = 2
-LAG = 2
+LAG = 3
 
 FLOPS = 2 * TOKENS * CHANNELS * CHANNELS + 2 * TOKENS * TOKENS * CHANNELS
-
-
-def quantise(nc, pool, grouped, label):
-    codes = pool.tile([P, HALF], U32, name="%s_codes" % label, align_bytes=64)
-    scales = pool.tile([P, HALF], U8, name="%s_scales" % label, align_bytes=64)
-    nc.vector.quantize_mx(out=codes[:].bitcast(FP8X4), scales=scales[:], in_=grouped[:])
-    return codes, scales
-
-
-def interleave_planes(nc, pool, planes, label):
-    grouped = pool.tile([P, HALF * PACK], BF16, name="%s_grouped" % label, align_bytes=64)
-    nc.vector.tensor_copy(
-        out=grouped[:].rearrange("p (c i t) -> p c t i", i=4, t=PACK),
-        in_=planes[:].rearrange("p t (c i) -> p c t i", i=4),
-    )
-    return grouped
-
-
-def channels_to_partitions(nc, pool, psum, identity, rows, label):
-    row_words = rows[:].bitcast(F32).rearrange("p (a w u) -> p a u w", a=PACK, u=WORD_PAIR)
-    grouped = pool.tile([P, HALF * PACK], BF16, name="%s_grouped" % label, align_bytes=64)
-    grouped_words = grouped[:].bitcast(F32).rearrange("p (a r u) -> p a r u", a=PACK, u=WORD_PAIR)
-    tiles_per_bank = 2
-    for first in range(0, PACK, tiles_per_bank):
-        bank = psum.tile([P, HALF], F32, tag="bank")
-        flipped = bank[:].rearrange("p (a u r) -> p a u r", a=tiles_per_bank, u=WORD_PAIR)
-        for a in range(tiles_per_bank):
-            for u in range(WORD_PAIR):
-                nc.tensor.transpose(flipped[:, a, u, :], row_words[:, first + a, u, :], identity[:])
-        nc.scalar.copy(
-            out=grouped_words[:, first : first + tiles_per_bank],
-            in_=flipped.rearrange("p a u r -> p a r u"),
-        )
-    return grouped
 
 
 def tile_visionattention_pa_kernel(tc, x, Wq, bq, k, out):
@@ -70,23 +37,32 @@ def tile_visionattention_pa_kernel(tc, x, Wq, bq, k, out):
 
     with ExitStack() as ctx:
         keep = ctx.enter_context(tc.tile_pool(name="keep", bufs=1))
-        rows_pool = ctx.enter_context(tc.tile_pool(name="rows", bufs=LAG + 3))
+        rows_pool = ctx.enter_context(tc.tile_pool(name="rows", bufs=TILES))
         psum = ctx.enter_context(tc.psum_pool(name="psum", bufs=8))
+
+        def half(h):
+            return slice(h * HALF, (h + 1) * HALF)
+
+        def load_x(h):
+            planes = keep.tile([P, PACK, HALF], BF16, name="x_planes%d" % h)
+            nc.sync.dma_start(
+                out=planes[:], in_=x_rows_dram[:, half(h)].rearrange("(p t) n -> p t n", t=PACK)
+            )
+            return planes
+
+        def load_k(h):
+            rows = keep.tile([P, PACK * CHANNELS], BF16, name="k_rows%d" % h)
+            nc.sync.dma_start(out=rows[:], in_=k_rows_dram[half(h), :].rearrange("(r a) c -> r (a c)", a=PACK))
+            return rows
 
         wq_rows = keep.tile([P, PACK * CHANNELS], BF16)
         nc.sync.dma_start(out=wq_rows[:], in_=Wq.rearrange("(r t) c -> r (t c)", t=PACK))
-        x_planes = []
-        k_rows = []
-        for h in range(HALVES):
-            cols = slice(h * HALF, (h + 1) * HALF)
-            x_half = keep.tile([P, PACK, HALF], BF16, name="x_planes%d" % h)
-            nc.sync.dma_start(
-                out=x_half[:], in_=x_rows_dram[:, cols].rearrange("(p t) n -> p t n", t=PACK)
-            )
-            x_planes.append(x_half)
-            k_half = keep.tile([P, PACK * CHANNELS], BF16, name="k_rows%d" % h)
-            nc.sync.dma_start(out=k_half[:], in_=k_rows_dram[cols, :].rearrange("(r a) c -> r (a c)", a=PACK))
-            k_rows.append(k_half)
+        x_planes = {}
+        k_rows = {}
+        x_planes[0] = load_x(0)
+        k_rows[0] = load_k(0)
+        x_planes[1] = load_x(1)
+        k_rows[1] = load_k(1)
         bq_raw = keep.tile([P, PACK], BF16)
         nc.scalar.dma_start(out=bq_raw[:], in_=bq.rearrange("(r t) -> r t", t=PACK))
 
@@ -98,42 +74,130 @@ def tile_visionattention_pa_kernel(tc, x, Wq, bq, k, out):
         bias = keep.tile([P, PACK], F32)
         nc.vector.tensor_scalar_mul(out=bias[:], in0=bq_raw[:], scalar1=INV_SQRT_CHANNELS)
 
-        wq_grouped = channels_to_partitions(nc, keep, psum, identity, wq_rows, "wq")
-        wq_codes, wq_scales = quantise(nc, keep, wq_grouped, "wq")
+        def packed_tile(width, label):
+            codes = keep.tile([P, width], U32, name="%s_codes" % label, align_bytes=64)
+            scales = keep.tile([P, width], U8, name="%s_scales" % label, align_bytes=64)
+            return codes, scales
 
-        x_mx = []
-        k_mx = []
-        for h in range(HALVES):
-            x_grouped = interleave_planes(nc, keep, x_planes[h], "x%d" % h)
-            x_mx.append(quantise(nc, keep, x_grouped, "x%d" % h))
-            k_grouped = channels_to_partitions(nc, keep, psum, identity, k_rows[h], "k%d" % h)
-            k_mx.append(quantise(nc, keep, k_grouped, "k%d" % h))
+        def quantise(packed, cols, grouped):
+            codes, scales = packed
+            nc.vector.quantize_mx(out=codes[:, cols].bitcast(FP8X4), scales=scales[:, cols], in_=grouped)
 
-        q_mx = []
-        for h in range(HALVES):
-            x_codes, x_scales = x_mx[h]
-            q_planes = keep.tile([P, PACK, HALF], BF16, name="q_planes%d" % h)
+        def grouped_tile(width, label):
+            return keep.tile([P, width * PACK], BF16, name="%s_grouped" % label, align_bytes=64)
+
+        def multiply(out, stationary, stationary_cols, moving, moving_cols):
+            nc.tensor.matmul_mx(
+                out=out,
+                lhsT=stationary[0][:, stationary_cols].bitcast(FP8X4),
+                lhsT_scale=stationary[1][:, stationary_cols],
+                rhs=moving[0][:, moving_cols].bitcast(FP8X4),
+                rhs_scale=moving[1][:, moving_cols],
+                start=True,
+                stop=True,
+            )
+
+        flipped = {}
+
+        def flip(label, rows, pair):
+            row_words = rows[:].bitcast(F32).rearrange("p (a w u) -> p a u w", a=PACK, u=WORD_PAIR)
+            bank = psum.tile([P, HALF], F32, tag="bank")
+            views = bank[:].rearrange("p (a u r) -> p a u r", a=2, u=WORD_PAIR)
+            for a in range(2):
+                for u in range(WORD_PAIR):
+                    nc.tensor.transpose(views[:, a, u, :], row_words[:, 2 * pair + a, u, :], identity[:])
+            flipped[label, pair] = views
+
+        def unflip(copy, label, pair):
+            words = grouped[label][:].bitcast(F32).rearrange("p (a r u) -> p a r u", a=PACK, u=WORD_PAIR)
+            copy(
+                out=words[:, 2 * pair : 2 * pair + 2],
+                in_=flipped[label, pair].rearrange("p a u r -> p a r u"),
+            )
+
+        def quantise_rows(label, pair):
+            quantise(
+                packed[label],
+                slice(pair * CHUNK, (pair + 1) * CHUNK),
+                grouped[label][:, pair * CHUNK * PACK : (pair + 1) * CHUNK * PACK],
+            )
+
+        def interleave(copy, planes, wide):
+            copy(
+                out=wide.rearrange("p (c i t) -> p c t i", i=4, t=PACK),
+                in_=planes.rearrange("p t (c i) -> p c t i", i=4),
+            )
+
+        def gpsimd_copy(out, in_):
+            nc.gpsimd.tensor_scalar(out=out, in0=in_, scalar1=1.0, scalar2=0.0, op0=ALU.mult, op1=ALU.add)
+
+        def interleave_x(copy, c):
+            first = (c * CHUNK) % HALF
+            interleave(copy, x_planes[(c * CHUNK) // HALF][:, :, first : first + CHUNK], grouped["x", c][:])
+
+        grouped = {}
+        packed = {}
+        for label in ("wq", "k0", "k1"):
+            grouped[label] = grouped_tile(HALF, label)
+            packed[label] = packed_tile(HALF, label)
+        for c in range(CHUNKS):
+            for kind in ("x", "q"):
+                grouped[kind, c] = grouped_tile(CHUNK, "%s%d" % (kind, c))
+                packed[kind, c] = packed_tile(CHUNK, "%s%d" % (kind, c))
+
+        def quantise_chunk(kind, c):
+            quantise(packed[kind, c], slice(0, CHUNK), grouped[kind, c][:])
+
+        q_banks = {}
+
+        def project_tile(g):
+            bank = psum.tile([P, HALF], F32, tag="bank")
+            c, first = (g * P) // CHUNK, (g * P) % CHUNK
             for t in range(PACK):
-                out_channels = slice(t * P, (t + 1) * P)
-                bank = psum.tile([P, HALF], F32, tag="bank")
-                nc.tensor.matmul_mx(
-                    out=bank[:],
-                    lhsT=wq_codes[:, out_channels].bitcast(FP8X4),
-                    lhsT_scale=wq_scales[:, out_channels],
-                    rhs=x_codes[:].bitcast(FP8X4),
-                    rhs_scale=x_scales[:],
-                    start=True,
-                    stop=True,
+                multiply(
+                    bank[:, t * P : (t + 1) * P], packed["wq"], slice(t * P, (t + 1) * P),
+                    packed["x", c], slice(first, first + P),
                 )
+            q_banks[g] = bank
+
+        def mix_tile(g):
+            c, first = (g * P) // CHUNK, ((g * P) % CHUNK) * PACK
+            nc.vector.scalar_tensor_tensor(
+                out=grouped["q", c][:, first : first + P * PACK].rearrange("p (n t) -> p n t", t=PACK),
+                in0=q_banks[g][:].rearrange("p (t n) -> p n t", t=PACK),
+                scalar=INV_SQRT_CHANNELS,
+                in1=bias[:].unsqueeze(1).to_broadcast([P, P, PACK]),
+                op0=ALU.mult,
+                op1=ALU.add,
+            )
+
+        q_planes = {}
+
+        def project_chunk(c):
+            q_planes[c] = keep.tile([P, PACK, CHUNK], BF16, name="q_planes%d" % c)
+            for pair in range(2):
+                bank = psum.tile([P, HALF], F32, tag="bank")
+                for e in range(2):
+                    t = 2 * pair + e
+                    multiply(
+                        bank[:, e * CHUNK : (e + 1) * CHUNK], packed["wq"], slice(t * P, (t + 1) * P),
+                        packed["x", c], slice(0, CHUNK),
+                    )
+                q_banks[c, pair] = bank
+
+        def empty_chunk(c, pair):
+            for e in range(2):
+                t = 2 * pair + e
                 nc.scalar.activation(
-                    out=q_planes[:, t, :],
-                    in_=bank[:],
+                    out=q_planes[c][:, t, :],
+                    in_=q_banks[c, pair][:, e * CHUNK : (e + 1) * CHUNK],
                     func=ACT.Identity,
                     bias=bias[:, t : t + 1],
                     scale=INV_SQRT_CHANNELS,
                 )
-            q_grouped = interleave_planes(nc, keep, q_planes, "q%d" % h)
-            q_mx.append(quantise(nc, keep, q_grouped, "q%d" % h))
+
+        def mix_chunk(copy, c):
+            interleave(copy, q_planes[c][:], grouped["q", c][:])
 
         scores = {}
         maxes = {}
@@ -144,30 +208,18 @@ def tile_visionattention_pa_kernel(tc, x, Wq, bq, k, out):
         inv_sum = {}
 
         def score(g):
-            q_codes, q_scales = q_mx[(g * P) // HALF]
-            tokens = slice((g * P) % HALF, (g * P) % HALF + P)
+            c, first = (g * P) // CHUNK, (g * P) % CHUNK
             scores[g] = []
             for h in range(HALVES):
-                k_codes, k_scales = k_mx[h]
                 bank = psum.tile([P, HALF], F32, tag="bank")
-                nc.tensor.matmul_mx(
-                    out=bank[:],
-                    lhsT=q_codes[:, tokens].bitcast(FP8X4),
-                    lhsT_scale=q_scales[:, tokens],
-                    rhs=k_codes[:].bitcast(FP8X4),
-                    rhs_scale=k_scales[:],
-                    start=True,
-                    stop=True,
-                )
+                multiply(bank[:], packed["q", c], slice(first, first + P), packed["k%d" % h], slice(0, HALF))
                 scores[g].append(bank)
 
         def bank_maximum(g, h):
             if h == 0:
                 bank_maxes = rows_pool.tile([P, HALVES], F32, tag="maxes")
                 maxes[g] = bank_maxes
-            nc.vector.tensor_reduce(
-                out=maxes[g][:, h : h + 1], in_=scores[g][h][:], axis=AXIS.X, op=ALU.max
-            )
+            nc.vector.tensor_reduce(out=maxes[g][:, h : h + 1], in_=scores[g][h][:], axis=AXIS.X, op=ALU.max)
 
         def negate_maximum(g):
             minus = rows_pool.tile([P, 1], F32, tag="neg_max")
@@ -179,7 +231,7 @@ def tile_visionattention_pa_kernel(tc, x, Wq, bq, k, out):
             bank_sums = rows_pool.tile([P, HALVES], F32, tag="sums")
             for h in range(HALVES):
                 nc.scalar.activation(
-                    out=row_tile[:, h * HALF : (h + 1) * HALF].rearrange("p (r a) -> p r a", a=PACK),
+                    out=row_tile[:, half(h)].rearrange("p (r a) -> p r a", a=PACK),
                     in_=scores[g][h][:].rearrange("p (a r) -> p r a", a=PACK),
                     func=ACT.Exp,
                     bias=neg_max[g][:, 0:1],
@@ -199,45 +251,104 @@ def tile_visionattention_pa_kernel(tc, x, Wq, bq, k, out):
             nc.vector.reciprocal(out=inverse[:], in_=row_sum[g][:])
             inv_sum[g] = inverse
 
-        def scale_and_store(g):
-            rows = slice(g * P, (g + 1) * P)
-            if g < TILES - LAG:
-                nc.gpsimd.tensor_scalar(
-                    out=probs[g][:],
-                    in0=probs[g][:],
-                    scalar1=inv_sum[g][:, 0:1],
-                    scalar2=0.0,
-                    op0=ALU.mult,
-                    op1=ALU.add,
-                )
-                nc.sync.dma_start(out=out_rows_dram[rows, :], in_=probs[g][:])
-            else:
-                for h in range(HALVES):
-                    cols = slice(h * HALF, (h + 1) * HALF)
-                    nc.vector.tensor_scalar_mul(
-                        out=probs[g][:, cols], in0=probs[g][:, cols], scalar1=inv_sum[g][:, 0:1]
-                    )
-                    nc.sync.dma_start(out=out_rows_dram[rows, cols], in_=probs[g][:, cols])
+        def store(g, cols):
+            nc.sync.dma_start(out=out_rows_dram[g * P : (g + 1) * P, cols], in_=probs[g][:, cols])
 
-        def is_tile(g):
-            return 0 <= g < TILES
+        def scale_on_gpsimd(g):
+            nc.gpsimd.tensor_scalar(
+                out=probs[g][:], in0=probs[g][:], scalar1=inv_sum[g][:, 0:1], scalar2=0.0,
+                op0=ALU.mult, op1=ALU.add,
+            )
+            store(g, slice(0, TOKENS))
+
+        def scale_on_vector(g, cols):
+            nc.vector.tensor_scalar_mul(out=probs[g][:, cols], in0=probs[g][:, cols], scalar1=inv_sum[g][:, 0:1])
+            store(g, cols)
+
+        def scale_on_scalar(g, cols):
+            nc.scalar.activation(
+                out=probs[g][:, cols], in_=probs[g][:, cols], func=ACT.Copy, scale=inv_sum[g][:, 0:1]
+            )
+            store(g, cols)
+
+        on_scalar = nc.scalar.copy
+        on_vector = nc.vector.tensor_copy
 
         with tc.manual_schedule():
-            for g in range(SCORE_LEAD):
-                score(g)
-            for s in range(TILES + LAG):
-                if is_tile(s + SCORE_LEAD):
-                    score(s + SCORE_LEAD)
-                if is_tile(s):
-                    bank_maximum(s, 0)
-                if is_tile(s - LAG):
-                    add_sums(s - LAG)
-                if is_tile(s):
-                    bank_maximum(s, 1)
-                if is_tile(s - LAG):
-                    invert_sum(s - LAG)
-                if is_tile(s):
-                    negate_maximum(s)
-                    exponentials(s)
-                if is_tile(s - LAG):
-                    scale_and_store(s - LAG)
+            flip("wq", wq_rows, 0)
+            flip("wq", wq_rows, 1)
+            unflip(on_vector, "wq", 0)
+            unflip(on_scalar, "wq", 1)
+            interleave_x(on_vector, 0)
+            interleave_x(on_scalar, 1)
+            quantise_rows("wq", 0)
+            quantise_rows("wq", 1)
+            quantise_chunk("x", 0)
+            flip("k0", k_rows[0], 0)
+            flip("k0", k_rows[0], 1)
+            project_tile(0)
+            project_tile(1)
+            interleave_x(gpsimd_copy, 2)
+            quantise_chunk("x", 1)
+            unflip(on_vector, "k0", 0)
+            unflip(on_scalar, "k0", 1)
+            interleave_x(on_scalar, 3)
+            mix_tile(0)
+            mix_tile(1)
+            project_chunk(1)
+            flip("k1", k_rows[1], 0)
+            flip("k1", k_rows[1], 1)
+            empty_chunk(1, 0)
+            unflip(on_scalar, "k1", 0)
+            unflip(on_scalar, "k1", 1)
+            empty_chunk(1, 1)
+            quantise_rows("k0", 0)
+            quantise_chunk("q", 0)
+            quantise_rows("k0", 1)
+            quantise_chunk("x", 2)
+            quantise_rows("k1", 0)
+            project_chunk(2)
+            quantise_chunk("x", 3)
+            quantise_rows("k1", 1)
+            score(0)
+            score(1)
+            project_chunk(3)
+            empty_chunk(2, 0)
+            empty_chunk(2, 1)
+            mix_chunk(on_vector, 1)
+            bank_maximum(0, 0)
+            quantise_chunk("q", 1)
+            bank_maximum(0, 1)
+            empty_chunk(3, 0)
+            empty_chunk(3, 1)
+            score(2)
+            for g in range(1, TILES):
+                bank_maximum(g, 0)
+                negate_maximum(g - 1)
+                exponentials(g - 1)
+                if g == 1:
+                    mix_chunk(on_vector, 2)
+                if g == 2:
+                    quantise_chunk("q", 2)
+                    mix_chunk(on_vector, 3)
+                if g == 3:
+                    quantise_chunk("q", 3)
+                if g >= LAG:
+                    add_sums(g - LAG)
+                bank_maximum(g, 1)
+                if g >= LAG:
+                    invert_sum(g - LAG)
+                    scale_on_gpsimd(g - LAG)
+                if g + 2 < TILES:
+                    score(g + 2)
+            negate_maximum(TILES - 1)
+            exponentials(TILES - 1)
+            for g in range(TILES - LAG, TILES - 1):
+                add_sums(g)
+                invert_sum(g)
+                scale_on_vector(g, half(0))
+                scale_on_vector(g, half(1))
+            add_sums(TILES - 1)
+            invert_sum(TILES - 1)
+            scale_on_vector(TILES - 1, half(0))
+            scale_on_scalar(TILES - 1, half(1))

@@ -24,7 +24,7 @@ CHUNKS = TOKENS // CHUNK
 WORD_PAIR = 2
 INV_SQRT_CHANNELS = 1.0 / math.sqrt(CHANNELS)
 TILES = TOKENS // P
-LAG = 3
+GPSIMD_TILES = 5
 
 FLOPS = 2 * TOKENS * CHANNELS * CHANNELS + 2 * TOKENS * TOKENS * CHANNELS
 
@@ -55,11 +55,15 @@ def tile_visionattention_pa_kernel(tc, x, Wq, bq, k, out):
             nc.sync.dma_start(out=rows[:], in_=k_rows_dram[half(h), :].rearrange("(r a) c -> r (a c)", a=PACK))
             return rows
 
-        wq_rows = keep.tile([P, PACK * CHANNELS], BF16)
-        nc.sync.dma_start(out=wq_rows[:], in_=Wq.rearrange("(r t) c -> r (t c)", t=PACK))
         x_planes = {}
         k_rows = {}
         x_planes[0] = load_x(0)
+        wq_rows = keep.tile([P, PACK * CHANNELS], BF16)
+        for pair in range(2):
+            nc.sync.dma_start(
+                out=wq_rows[:, pair * 2 * CHANNELS : (pair + 1) * 2 * CHANNELS],
+                in_=Wq.rearrange("(r s) c -> r (s c)", s=PACK)[:, pair * 2 * CHANNELS : (pair + 1) * 2 * CHANNELS],
+            )
         k_rows[0] = load_k(0)
         x_planes[1] = load_x(1)
         k_rows[1] = load_k(1)
@@ -71,6 +75,8 @@ def tile_visionattention_pa_kernel(tc, x, Wq, bq, k, out):
         warm = keep.tile([P, 1], F32)
         nc.vector.memset(warm[:], 0.0)
         nc.scalar.activation(out=warm[:], in_=warm[:], func=ACT.Exp)
+        minus_one = keep.tile([P, 1], F32)
+        nc.gpsimd.memset(minus_one[:], -1.0)
         bias = keep.tile([P, PACK], F32)
         nc.vector.tensor_scalar_mul(out=bias[:], in0=bq_raw[:], scalar1=INV_SQRT_CHANNELS)
 
@@ -251,6 +257,13 @@ def tile_visionattention_pa_kernel(tc, x, Wq, bq, k, out):
             nc.vector.reciprocal(out=inverse[:], in_=row_sum[g][:])
             inv_sum[g] = inverse
 
+        def invert_sum_on_gpsimd(g):
+            total = rows_pool.tile([P, 1], F32, tag="row_sum")
+            nc.gpsimd.tensor_tensor(out=total[:], in0=sums[g][:, 0:1], in1=sums[g][:, 1:2], op=ALU.add)
+            inverse = rows_pool.tile([P, 1], F32, tag="inv_sum")
+            nc.gpsimd.tensor_tensor(out=inverse[:], in0=total[:], in1=minus_one[:], op=ALU.pow)
+            inv_sum[g] = inverse
+
         def store(g, cols):
             nc.sync.dma_start(out=out_rows_dram[g * P : (g + 1) * P, cols], in_=probs[g][:, cols])
 
@@ -275,21 +288,21 @@ def tile_visionattention_pa_kernel(tc, x, Wq, bq, k, out):
         on_vector = nc.vector.tensor_copy
 
         with tc.manual_schedule():
+            interleave_x(gpsimd_copy, 0)
+            interleave_x(on_scalar, 1)
             flip("wq", wq_rows, 0)
             flip("wq", wq_rows, 1)
-            unflip(on_vector, "wq", 0)
-            unflip(on_scalar, "wq", 1)
-            interleave_x(on_vector, 0)
-            interleave_x(on_scalar, 1)
+            unflip(on_scalar, "wq", 0)
+            quantise_chunk("x", 0)
+            unflip(on_vector, "wq", 1)
             quantise_rows("wq", 0)
             quantise_rows("wq", 1)
-            quantise_chunk("x", 0)
+            quantise_chunk("x", 1)
             flip("k0", k_rows[0], 0)
             flip("k0", k_rows[0], 1)
             project_tile(0)
             project_tile(1)
             interleave_x(gpsimd_copy, 2)
-            quantise_chunk("x", 1)
             unflip(on_vector, "k0", 0)
             unflip(on_scalar, "k0", 1)
             interleave_x(on_scalar, 3)
@@ -302,53 +315,53 @@ def tile_visionattention_pa_kernel(tc, x, Wq, bq, k, out):
             unflip(on_scalar, "k1", 0)
             unflip(on_scalar, "k1", 1)
             empty_chunk(1, 1)
+            mix_chunk(gpsimd_copy, 1)
             quantise_rows("k0", 0)
-            quantise_chunk("q", 0)
             quantise_rows("k0", 1)
+            quantise_chunk("q", 0)
             quantise_chunk("x", 2)
-            quantise_rows("k1", 0)
             project_chunk(2)
-            quantise_chunk("x", 3)
-            quantise_rows("k1", 1)
-            score(0)
-            score(1)
-            project_chunk(3)
             empty_chunk(2, 0)
             empty_chunk(2, 1)
-            mix_chunk(on_vector, 1)
+            mix_chunk(gpsimd_copy, 2)
+            quantise_rows("k1", 0)
+            quantise_rows("k1", 1)
+            score(0)
+            quantise_chunk("x", 3)
+            project_chunk(3)
+            score(1)
             bank_maximum(0, 0)
-            quantise_chunk("q", 1)
             bank_maximum(0, 1)
+            bank_maximum(1, 0)
+            negate_maximum(0)
             empty_chunk(3, 0)
+            exponentials(0)
             empty_chunk(3, 1)
+            mix_chunk(gpsimd_copy, 3)
+            bank_maximum(1, 1)
+            quantise_chunk("q", 1)
             score(2)
-            for g in range(1, TILES):
+            for g in range(2, TILES):
                 bank_maximum(g, 0)
                 negate_maximum(g - 1)
                 exponentials(g - 1)
-                if g == 1:
-                    mix_chunk(on_vector, 2)
+                bank_maximum(g, 1)
                 if g == 2:
                     quantise_chunk("q", 2)
-                    mix_chunk(on_vector, 3)
                 if g == 3:
                     quantise_chunk("q", 3)
-                if g >= LAG:
-                    add_sums(g - LAG)
-                bank_maximum(g, 1)
-                if g >= LAG:
-                    invert_sum(g - LAG)
-                    scale_on_gpsimd(g - LAG)
-                if g + 2 < TILES:
-                    score(g + 2)
+                if g + 1 < TILES:
+                    score(g + 1)
+                if g - 2 < GPSIMD_TILES:
+                    invert_sum_on_gpsimd(g - 2)
+                    scale_on_gpsimd(g - 2)
             negate_maximum(TILES - 1)
             exponentials(TILES - 1)
-            for g in range(TILES - LAG, TILES - 1):
+            for g in range(GPSIMD_TILES, TILES):
                 add_sums(g)
                 invert_sum(g)
                 scale_on_vector(g, half(0))
-                scale_on_vector(g, half(1))
-            add_sums(TILES - 1)
-            invert_sum(TILES - 1)
-            scale_on_vector(TILES - 1, half(0))
-            scale_on_scalar(TILES - 1, half(1))
+                if g == TILES - 1:
+                    scale_on_scalar(g, half(1))
+                else:
+                    scale_on_vector(g, half(1))

@@ -24,7 +24,7 @@ CHUNKS = TOKENS // CHUNK
 WORD_PAIR = 2
 INV_SQRT_CHANNELS = 1.0 / math.sqrt(CHANNELS)
 TILES = TOKENS // P
-GPSIMD_TILES = 5
+GPSIMD_TILES = 6
 
 FLOPS = 2 * TOKENS * CHANNELS * CHANNELS + 2 * TOKENS * TOKENS * CHANNELS
 
@@ -75,8 +75,6 @@ def tile_visionattention_pa_kernel(tc, x, Wq, bq, k, out):
         warm = keep.tile([P, 1], F32)
         nc.vector.memset(warm[:], 0.0)
         nc.scalar.activation(out=warm[:], in_=warm[:], func=ACT.Exp)
-        minus_one = keep.tile([P, 1], F32)
-        nc.gpsimd.memset(minus_one[:], -1.0)
         bias = keep.tile([P, PACK], F32)
         nc.vector.tensor_scalar_mul(out=bias[:], in0=bq_raw[:], scalar1=INV_SQRT_CHANNELS)
 
@@ -133,9 +131,6 @@ def tile_visionattention_pa_kernel(tc, x, Wq, bq, k, out):
                 out=wide.rearrange("p (c i t) -> p c t i", i=4, t=PACK),
                 in_=planes.rearrange("p t (c i) -> p c t i", i=4),
             )
-
-        def gpsimd_copy(out, in_):
-            nc.gpsimd.tensor_scalar(out=out, in0=in_, scalar1=1.0, scalar2=0.0, op0=ALU.mult, op1=ALU.add)
 
         def interleave_x(copy, c):
             first = (c * CHUNK) % HALF
@@ -257,13 +252,6 @@ def tile_visionattention_pa_kernel(tc, x, Wq, bq, k, out):
             nc.vector.reciprocal(out=inverse[:], in_=row_sum[g][:])
             inv_sum[g] = inverse
 
-        def invert_sum_on_gpsimd(g):
-            total = rows_pool.tile([P, 1], F32, tag="row_sum")
-            nc.gpsimd.tensor_tensor(out=total[:], in0=sums[g][:, 0:1], in1=sums[g][:, 1:2], op=ALU.add)
-            inverse = rows_pool.tile([P, 1], F32, tag="inv_sum")
-            nc.gpsimd.tensor_tensor(out=inverse[:], in0=total[:], in1=minus_one[:], op=ALU.pow)
-            inv_sum[g] = inverse
-
         def store(g, cols):
             nc.sync.dma_start(out=out_rows_dram[g * P : (g + 1) * P, cols], in_=probs[g][:, cols])
 
@@ -288,73 +276,76 @@ def tile_visionattention_pa_kernel(tc, x, Wq, bq, k, out):
         on_vector = nc.vector.tensor_copy
 
         with tc.manual_schedule():
-            interleave_x(gpsimd_copy, 0)
+            interleave_x(on_vector, 0)
             interleave_x(on_scalar, 1)
+            quantise_chunk("x", 0)
+            quantise_chunk("x", 1)
             flip("wq", wq_rows, 0)
             flip("wq", wq_rows, 1)
-            unflip(on_scalar, "wq", 0)
-            quantise_chunk("x", 0)
-            unflip(on_vector, "wq", 1)
+            unflip(on_vector, "wq", 0)
+            unflip(on_scalar, "wq", 1)
             quantise_rows("wq", 0)
             quantise_rows("wq", 1)
-            quantise_chunk("x", 1)
             flip("k0", k_rows[0], 0)
             flip("k0", k_rows[0], 1)
             project_tile(0)
             project_tile(1)
-            interleave_x(gpsimd_copy, 2)
-            unflip(on_vector, "k0", 0)
+            unflip(on_scalar, "k0", 0)
+            interleave_x(on_scalar, 2)
+            interleave_x(on_vector, 3)
             unflip(on_scalar, "k0", 1)
-            interleave_x(on_scalar, 3)
             mix_tile(0)
             mix_tile(1)
             project_chunk(1)
-            flip("k1", k_rows[1], 0)
-            flip("k1", k_rows[1], 1)
-            empty_chunk(1, 0)
-            unflip(on_scalar, "k1", 0)
-            unflip(on_scalar, "k1", 1)
-            empty_chunk(1, 1)
-            mix_chunk(gpsimd_copy, 1)
+            for pair in range(2):
+                flip("k1", k_rows[1], pair)
+                unflip(on_scalar, "k1", pair)
+            quantise_chunk("x", 3)
+            quantise_chunk("q", 0)
             quantise_rows("k0", 0)
             quantise_rows("k0", 1)
-            quantise_chunk("q", 0)
             quantise_chunk("x", 2)
-            project_chunk(2)
-            empty_chunk(2, 0)
-            empty_chunk(2, 1)
-            mix_chunk(gpsimd_copy, 2)
+            empty_chunk(1, 0)
+            empty_chunk(1, 1)
             quantise_rows("k1", 0)
             quantise_rows("k1", 1)
+            project_chunk(2)
             score(0)
-            quantise_chunk("x", 3)
-            project_chunk(3)
-            score(1)
+            empty_chunk(2, 0)
+            empty_chunk(2, 1)
             bank_maximum(0, 0)
             bank_maximum(0, 1)
-            bank_maximum(1, 0)
             negate_maximum(0)
-            empty_chunk(3, 0)
             exponentials(0)
+            mix_chunk(on_vector, 1)
+            score(1)
+            project_chunk(3)
+            empty_chunk(3, 0)
             empty_chunk(3, 1)
-            mix_chunk(gpsimd_copy, 3)
-            bank_maximum(1, 1)
+            bank_maximum(1, 0)
             quantise_chunk("q", 1)
+            bank_maximum(1, 1)
             score(2)
             for g in range(2, TILES):
-                bank_maximum(g, 0)
+                if g == 2:
+                    mix_chunk(on_vector, 2)
                 negate_maximum(g - 1)
                 exponentials(g - 1)
-                bank_maximum(g, 1)
+                if g - 2 < GPSIMD_TILES:
+                    add_sums(g - 2)
+                bank_maximum(g, 0)
+                if g - 2 < GPSIMD_TILES:
+                    invert_sum(g - 2)
+                    scale_on_gpsimd(g - 2)
                 if g == 2:
                     quantise_chunk("q", 2)
                 if g == 3:
                     quantise_chunk("q", 3)
+                bank_maximum(g, 1)
+                if g == 2:
+                    mix_chunk(on_vector, 3)
                 if g + 1 < TILES:
                     score(g + 1)
-                if g - 2 < GPSIMD_TILES:
-                    invert_sum_on_gpsimd(g - 2)
-                    scale_on_gpsimd(g - 2)
             negate_maximum(TILES - 1)
             exponentials(TILES - 1)
             for g in range(GPSIMD_TILES, TILES):

@@ -24,7 +24,7 @@ CHUNKS = TOKENS // CHUNK
 WORD_PAIR = 2
 INV_SQRT_CHANNELS = 1.0 / math.sqrt(CHANNELS)
 TILES = TOKENS // P
-GPSIMD_TILES = 6
+GPSIMD_TILES = 5
 
 FLOPS = 2 * TOKENS * CHANNELS * CHANNELS + 2 * TOKENS * TOKENS * CHANNELS
 
@@ -291,65 +291,66 @@ def tile_visionattention_pa_kernel(tc, x, Wq, bq, k, out):
             project_tile(0)
             project_tile(1)
             unflip(on_scalar, "k0", 0)
-            interleave_x(on_scalar, 2)
-            interleave_x(on_vector, 3)
             unflip(on_scalar, "k0", 1)
+            interleave_x(on_vector, 2)
+            interleave_x(on_scalar, 3)
             mix_tile(0)
             mix_tile(1)
             project_chunk(1)
             for pair in range(2):
                 flip("k1", k_rows[1], pair)
                 unflip(on_scalar, "k1", pair)
-            quantise_chunk("x", 3)
-            quantise_chunk("q", 0)
+            quantise_chunk("x", 2)
             quantise_rows("k0", 0)
             quantise_rows("k0", 1)
-            quantise_chunk("x", 2)
-            empty_chunk(1, 0)
-            empty_chunk(1, 1)
+            quantise_chunk("q", 0)
+            quantise_chunk("x", 3)
             quantise_rows("k1", 0)
             quantise_rows("k1", 1)
             project_chunk(2)
             score(0)
-            empty_chunk(2, 0)
-            empty_chunk(2, 1)
+            project_chunk(3)
+            score(1)
+            for c in range(1, CHUNKS):
+                empty_chunk(c, 0)
+                empty_chunk(c, 1)
+            mix_chunk(on_vector, 1)
             bank_maximum(0, 0)
             bank_maximum(0, 1)
+            quantise_chunk("q", 1)
             negate_maximum(0)
             exponentials(0)
-            mix_chunk(on_vector, 1)
-            score(1)
-            project_chunk(3)
-            empty_chunk(3, 0)
-            empty_chunk(3, 1)
             bank_maximum(1, 0)
-            quantise_chunk("q", 1)
+            mix_chunk(on_vector, 2)
             bank_maximum(1, 1)
+            quantise_chunk("q", 2)
+            negate_maximum(1)
+            exponentials(1)
             score(2)
-            for g in range(2, TILES):
-                if g == 2:
-                    mix_chunk(on_vector, 2)
+            mix_chunk(on_vector, 3)
+            add_sums(0)
+            bank_maximum(2, 0)
+            quantise_chunk("q", 3)
+            invert_sum(0)
+            scale_on_gpsimd(0)
+            bank_maximum(2, 1)
+            score(3)
+            for g in range(3, TILES):
                 negate_maximum(g - 1)
                 exponentials(g - 1)
-                if g - 2 < GPSIMD_TILES:
-                    add_sums(g - 2)
                 bank_maximum(g, 0)
+                add_sums(g - 2)
+                bank_maximum(g, 1)
                 if g - 2 < GPSIMD_TILES:
                     invert_sum(g - 2)
                     scale_on_gpsimd(g - 2)
-                if g == 2:
-                    quantise_chunk("q", 2)
-                if g == 3:
-                    quantise_chunk("q", 3)
-                bank_maximum(g, 1)
-                if g == 2:
-                    mix_chunk(on_vector, 3)
                 if g + 1 < TILES:
                     score(g + 1)
             negate_maximum(TILES - 1)
             exponentials(TILES - 1)
             for g in range(GPSIMD_TILES, TILES):
-                add_sums(g)
+                if g > TILES - 3:
+                    add_sums(g)
                 invert_sum(g)
                 scale_on_vector(g, half(0))
                 if g == TILES - 1:

@@ -55,15 +55,15 @@ def tile_visionattention_pa_kernel(tc, x, Wq, bq, k, out):
             nc.sync.dma_start(out=rows[:], in_=k_rows_dram[half(h), :].rearrange("(r a) c -> r (a c)", a=PACK))
             return rows
 
-        x_planes = {}
-        k_rows = {}
-        x_planes[0] = load_x(0)
         wq_rows = keep.tile([P, PACK * CHANNELS], BF16)
         for pair in range(2):
             nc.sync.dma_start(
                 out=wq_rows[:, pair * 2 * CHANNELS : (pair + 1) * 2 * CHANNELS],
                 in_=Wq.rearrange("(r s) c -> r (s c)", s=PACK)[:, pair * 2 * CHANNELS : (pair + 1) * 2 * CHANNELS],
             )
+        x_planes = {}
+        k_rows = {}
+        x_planes[0] = load_x(0)
         k_rows[0] = load_k(0)
         x_planes[1] = load_x(1)
         k_rows[1] = load_k(1)
@@ -276,16 +276,16 @@ def tile_visionattention_pa_kernel(tc, x, Wq, bq, k, out):
         on_vector = nc.vector.tensor_copy
 
         with tc.manual_schedule():
-            interleave_x(on_vector, 0)
-            interleave_x(on_scalar, 1)
-            quantise_chunk("x", 0)
-            quantise_chunk("x", 1)
             flip("wq", wq_rows, 0)
             flip("wq", wq_rows, 1)
             unflip(on_vector, "wq", 0)
             unflip(on_scalar, "wq", 1)
+            interleave_x(on_vector, 0)
+            interleave_x(on_scalar, 1)
             quantise_rows("wq", 0)
             quantise_rows("wq", 1)
+            quantise_chunk("x", 0)
+            quantise_chunk("x", 1)
             flip("k0", k_rows[0], 0)
             flip("k0", k_rows[0], 1)
             project_tile(0)

@@ -75,6 +75,8 @@ def tile_visionattention_pa_kernel(tc, x, Wq, bq, k, out):
         warm = keep.tile([P, 1], F32)
         nc.vector.memset(warm[:], 0.0)
         nc.scalar.activation(out=warm[:], in_=warm[:], func=ACT.Exp)
+        zeros = keep.tile([P, HALF], BF16)
+        nc.vector.memset(zeros[:], 0.0)
         bias = keep.tile([P, PACK], F32)
         nc.vector.tensor_scalar_mul(out=bias[:], in0=bq_raw[:], scalar1=INV_SQRT_CHANNELS)
 
@@ -111,6 +113,11 @@ def tile_visionattention_pa_kernel(tc, x, Wq, bq, k, out):
                 for u in range(WORD_PAIR):
                     nc.tensor.transpose(views[:, a, u, :], row_words[:, 2 * pair + a, u, :], identity[:])
             flipped[label, pair] = views
+
+        def keep_busy(count):
+            bank = psum.tile([P, HALF], F32, tag="bank")
+            for repeat in range(count):
+                nc.tensor.matmul(bank[:], lhsT=zeros[:, 0:P], rhs=zeros[:], start=True, stop=True)
 
         def unflip(copy, label, pair):
             words = grouped[label][:].bitcast(F32).rearrange("p (a r u) -> p a r u", a=PACK, u=WORD_PAIR)
@@ -276,8 +283,10 @@ def tile_visionattention_pa_kernel(tc, x, Wq, bq, k, out):
         on_vector = nc.vector.tensor_copy
 
         with tc.manual_schedule():
+            keep_busy(4)
             flip("wq", wq_rows, 0)
             flip("wq", wq_rows, 1)
+            keep_busy(2)
             unflip(on_vector, "wq", 0)
             unflip(on_scalar, "wq", 1)
             interleave_x(on_vector, 0)

@@ -24,6 +24,7 @@ CHUNKS = TOKENS // CHUNK
 WORD_PAIR = 2
 INV_SQRT_CHANNELS = 1.0 / math.sqrt(CHANNELS)
 TILES = TOKENS // P
+VECTOR_COLUMNS = 640
 GPSIMD_TILES = 5
 
 FLOPS = 2 * TOKENS * CHANNELS * CHANNELS + 2 * TOKENS * TOKENS * CHANNELS
@@ -75,8 +76,9 @@ def tile_visionattention_pa_kernel(tc, x, Wq, bq, k, out):
         warm = keep.tile([P, 1], F32)
         nc.vector.memset(warm[:], 0.0)
         nc.scalar.activation(out=warm[:], in_=warm[:], func=ACT.Exp)
-        zeros = keep.tile([P, HALF], BF16)
-        nc.vector.memset(zeros[:], 0.0)
+        zero_words = keep.tile([P, HALF // 2], U32)
+        nc.vector.memset(zero_words[:], 0)
+        zeros = zero_words[:].bitcast(BF16)
         bias = keep.tile([P, PACK], F32)
         nc.vector.tensor_scalar_mul(out=bias[:], in0=bq_raw[:], scalar1=INV_SQRT_CHANNELS)
 
@@ -117,7 +119,7 @@ def tile_visionattention_pa_kernel(tc, x, Wq, bq, k, out):
         def keep_busy(count):
             bank = psum.tile([P, HALF], F32, tag="bank")
             for repeat in range(count):
-                nc.tensor.matmul(bank[:], lhsT=zeros[:, 0:P], rhs=zeros[:], start=True, stop=True)
+                nc.tensor.matmul(bank[:], lhsT=zeros[:, 0:P], rhs=zeros, start=True, stop=True)
 
         def unflip(copy, label, pair):
             words = grouped[label][:].bitcast(F32).rearrange("p (a r u) -> p a r u", a=PACK, u=WORD_PAIR)
@@ -350,8 +352,8 @@ def tile_visionattention_pa_kernel(tc, x, Wq, bq, k, out):
                 bank_maximum(g, 0)
                 add_sums(g - 2)
                 bank_maximum(g, 1)
+                invert_sum(g - 2)
                 if g - 2 < GPSIMD_TILES:
-                    invert_sum(g - 2)
                     scale_on_gpsimd(g - 2)
                 if g + 1 < TILES:
                     score(g + 1)
@@ -360,9 +362,10 @@ def tile_visionattention_pa_kernel(tc, x, Wq, bq, k, out):
             for g in range(GPSIMD_TILES, TILES):
                 if g > TILES - 3:
                     add_sums(g)
-                invert_sum(g)
-                scale_on_vector(g, half(0))
+                    invert_sum(g)
                 if g == TILES - 1:
-                    scale_on_scalar(g, half(1))
+                    scale_on_vector(g, slice(0, VECTOR_COLUMNS))
+                    scale_on_scalar(g, slice(VECTOR_COLUMNS, TOKENS))
                 else:
+                    scale_on_vector(g, half(0))
                     scale_on_vector(g, half(1))

@@ -331,6 +331,7 @@ def tile_visionattention_pa_kernel(tc, x, Wq, bq, k, out):
             quantise_chunk("q", 1)
             negate_maximum(0)
             exponentials(0)
+            mix_chunk(on_scalar, 3)
             bank_maximum(1, 0)
             mix_chunk(on_vector, 2)
             bank_maximum(1, 1)
@@ -338,7 +339,6 @@ def tile_visionattention_pa_kernel(tc, x, Wq, bq, k, out):
             negate_maximum(1)
             exponentials(1)
             score(2)
-            mix_chunk(on_vector, 3)
             add_sums(0)
             bank_maximum(2, 0)
             quantise_chunk("q", 3)

import math
from contextlib import ExitStack

import concourse.masks as masks
import concourse.mybir as mybir

F32 = mybir.dt.float32
BF16 = mybir.dt.bfloat16
U32 = mybir.dt.uint32
U8 = mybir.dt.uint8
FP8X4 = mybir.dt.float8_e4m3fn_x4
ACT = mybir.ActivationFunctionType
ALU = mybir.AluOpType
AXIS = mybir.AxisListType

P = 128
PACK = 4
CHANNELS = P * PACK
TOKENS = 1024
HALF = 512
HALVES = TOKENS // HALF
CHUNK = 256
CHUNKS = TOKENS // CHUNK
WORD_PAIR = 2
INV_SQRT_CHANNELS = 1.0 / math.sqrt(CHANNELS)
TILES = TOKENS // P
VECTOR_COLUMNS = 640
GPSIMD_TILES = 5

FLOPS = 2 * TOKENS * CHANNELS * CHANNELS + 2 * TOKENS * TOKENS * CHANNELS


def tile_visionattention_pa_kernel(tc, x, Wq, bq, k, out):
    nc = tc.nc
    x_rows_dram = x.rearrange("b c h w -> (b c) (h w)")
    k_rows_dram = k.flatten_outer_dims()
    out_rows_dram = out.flatten_outer_dims()

    with ExitStack() as ctx:
        keep = ctx.enter_context(tc.tile_pool(name="keep", bufs=1))
        rows_pool = ctx.enter_context(tc.tile_pool(name="rows", bufs=TILES))
        psum = ctx.enter_context(tc.psum_pool(name="psum", bufs=8))

        def half(h):
            return slice(h * HALF, (h + 1) * HALF)

        def load_x(h):
            planes = keep.tile([P, PACK, HALF], BF16, name="x_planes%d" % h)
            nc.sync.dma_start(
                out=planes[:], in_=x_rows_dram[:, half(h)].rearrange("(p t) n -> p t n", t=PACK)
            )
            return planes

        def load_k(h):
            rows = keep.tile([P, PACK * CHANNELS], BF16, name="k_rows%d" % h)
            nc.sync.dma_start(out=rows[:], in_=k_rows_dram[half(h), :].rearrange("(r a) c -> r (a c)", a=PACK))
            return rows

        wq_rows = keep.tile([P, PACK * CHANNELS], BF16)
        for pair in range(2):
            nc.sync.dma_start(
                out=wq_rows[:, pair * 2 * CHANNELS : (pair + 1) * 2 * CHANNELS],
                in_=Wq.rearrange("(r s) c -> r (s c)", s=PACK)[:, pair * 2 * CHANNELS : (pair + 1) * 2 * CHANNELS],
            )
        x_planes = {}
        k_rows = {}
        x_planes[0] = load_x(0)
        k_rows[0] = load_k(0)
        x_planes[1] = load_x(1)
        k_rows[1] = load_k(1)
        bq_raw = keep.tile([P, PACK], BF16)
        nc.scalar.dma_start(out=bq_raw[:], in_=bq.rearrange("(r t) -> r t", t=PACK))

        identity = keep.tile([P, P], F32)
        masks.make_identity(nc, identity[:])
        warm = keep.tile([P, 1], F32)
        nc.vector.memset(warm[:], 0.0)
        nc.scalar.activation(out=warm[:], in_=warm[:], func=ACT.Exp)
        zero_words = keep.tile([P, HALF // 2], U32)
        nc.vector.memset(zero_words[:], 0)
        zeros = zero_words[:].bitcast(BF16)
        bias = keep.tile([P, PACK], F32)
        nc.vector.tensor_scalar_mul(out=bias[:], in0=bq_raw[:], scalar1=INV_SQRT_CHANNELS)

        def packed_tile(width, label):
            codes = keep.tile([P, width], U32, name="%s_codes" % label, align_bytes=64)
            scales = keep.tile([P, width], U8, name="%s_scales" % label, align_bytes=64)
            return codes, scales

        def quantise(packed, cols, grouped):
            codes, scales = packed
            nc.vector.quantize_mx(out=codes[:, cols].bitcast(FP8X4), scales=scales[:, cols], in_=grouped)

        def grouped_tile(width, label):
            return keep.tile([P, width * PACK], BF16, name="%s_grouped" % label, align_bytes=64)

        def multiply(out, stationary, stationary_cols, moving, moving_cols):
            nc.tensor.matmul_mx(
                out=out,
                lhsT=stationary[0][:, stationary_cols].bitcast(FP8X4),
                lhsT_scale=stationary[1][:, stationary_cols],
                rhs=moving[0][:, moving_cols].bitcast(FP8X4),
                rhs_scale=moving[1][:, moving_cols],
                start=True,
                stop=True,
            )

        flipped = {}

        def flip(label, rows, pair):
            row_words = rows[:].bitcast(F32).rearrange("p (a w u) -> p a u w", a=PACK, u=WORD_PAIR)
            bank = psum.tile([P, HALF], F32, tag="bank")
            views = bank[:].rearrange("p (a u r) -> p a u r", a=2, u=WORD_PAIR)
            for a in range(2):
                for u in range(WORD_PAIR):
                    nc.tensor.transpose(views[:, a, u, :], row_words[:, 2 * pair + a, u, :], identity[:])
            flipped[label, pair] = views

        def keep_busy(count):
            bank = psum.tile([P, HALF], F32, tag="bank")
            for repeat in range(count):
                nc.tensor.matmul(bank[:], lhsT=zeros[:, 0:P], rhs=zeros, start=True, stop=True)

        def unflip(copy, label, pair):
            words = grouped[label][:].bitcast(F32).rearrange("p (a r u) -> p a r u", a=PACK, u=WORD_PAIR)
            copy(
                out=words[:, 2 * pair : 2 * pair + 2],
                in_=flipped[label, pair].rearrange("p a u r -> p a r u"),
            )

        def quantise_rows(label, pair):
            quantise(
                packed[label],
                slice(pair * CHUNK, (pair + 1) * CHUNK),
                grouped[label][:, pair * CHUNK * PACK : (pair + 1) * CHUNK * PACK],
            )

        def interleave(copy, planes, wide):
            copy(
                out=wide.rearrange("p (c i t) -> p c t i", i=4, t=PACK),
                in_=planes.rearrange("p t (c i) -> p c t i", i=4),
            )

        def interleave_x(copy, c):
            first = (c * CHUNK) % HALF
            interleave(copy, x_planes[(c * CHUNK) // HALF][:, :, first : first + CHUNK], grouped["x", c][:])

        grouped = {}
        packed = {}
        for label in ("wq", "k0", "k1"):
            grouped[label] = grouped_tile(HALF, label)
            packed[label] = packed_tile(HALF, label)
        for c in range(CHUNKS):
            for kind in ("x", "q"):
                grouped[kind, c] = grouped_tile(CHUNK, "%s%d" % (kind, c))
                packed[kind, c] = packed_tile(CHUNK, "%s%d" % (kind, c))

        def quantise_chunk(kind, c):
            quantise(packed[kind, c], slice(0, CHUNK), grouped[kind, c][:])

        q_banks = {}

        def project_tile(g):
            bank = psum.tile([P, HALF], F32, tag="bank")
            c, first = (g * P) // CHUNK, (g * P) % CHUNK
            for t in range(PACK):
                multiply(
                    bank[:, t * P : (t + 1) * P], packed["wq"], slice(t * P, (t + 1) * P),
                    packed["x", c], slice(first, first + P),
                )
            q_banks[g] = bank

        def mix_tile(g):
            c, first = (g * P) // CHUNK, ((g * P) % CHUNK) * PACK
            nc.vector.scalar_tensor_tensor(
                out=grouped["q", c][:, first : first + P * PACK].rearrange("p (n t) -> p n t", t=PACK),
                in0=q_banks[g][:].rearrange("p (t n) -> p n t", t=PACK),
                scalar=INV_SQRT_CHANNELS,
                in1=bias[:].unsqueeze(1).to_broadcast([P, P, PACK]),
                op0=ALU.mult,
                op1=ALU.add,
            )

        q_planes = {}

        def project_chunk(c):
            q_planes[c] = keep.tile([P, PACK, CHUNK], BF16, name="q_planes%d" % c)
            for pair in range(2):
                bank = psum.tile([P, HALF], F32, tag="bank")
                for e in range(2):
                    t = 2 * pair + e
                    multiply(
                        bank[:, e * CHUNK : (e + 1) * CHUNK], packed["wq"], slice(t * P, (t + 1) * P),
                        packed["x", c], slice(0, CHUNK),
                    )
                q_banks[c, pair] = bank

        def empty_chunk(c, pair):
            for e in range(2):
                t = 2 * pair + e
                nc.scalar.activation(
                    out=q_planes[c][:, t, :],
                    in_=q_banks[c, pair][:, e * CHUNK : (e + 1) * CHUNK],
                    func=ACT.Identity,
                    bias=bias[:, t : t + 1],
                    scale=INV_SQRT_CHANNELS,
                )

        def mix_chunk(copy, c):
            interleave(copy, q_planes[c][:], grouped["q", c][:])

        scores = {}
        maxes = {}
        neg_max = {}
        probs = {}
        sums = {}
        row_sum = {}
        inv_sum = {}

        def score(g):
            c, first = (g * P) // CHUNK, (g * P) % CHUNK
            scores[g] = []
            for h in range(HALVES):
                bank = psum.tile([P, HALF], F32, tag="bank")
                multiply(bank[:], packed["q", c], slice(first, first + P), packed["k%d" % h], slice(0, HALF))
                scores[g].append(bank)

        def bank_maximum(g, h):
            if h == 0:
                bank_maxes = rows_pool.tile([P, HALVES], F32, tag="maxes")
                maxes[g] = bank_maxes
            nc.vector.tensor_reduce(out=maxes[g][:, h : h + 1], in_=scores[g][h][:], axis=AXIS.X, op=ALU.max)

        def negate_maximum(g):
            minus = rows_pool.tile([P, 1], F32, tag="neg_max")
            nc.vector.tensor_reduce(out=minus[:], in_=maxes[g][:], axis=AXIS.X, op=ALU.max, negate=True)
            neg_max[g] = minus

        def exponentials(g):
            row_tile = rows_pool.tile([P, TOKENS], F32, tag="probs")
            bank_sums = rows_pool.tile([P, HALVES], F32, tag="sums")
            for h in range(HALVES):
                nc.scalar.activation(
                    out=row_tile[:, half(h)].rearrange("p (r a) -> p r a", a=PACK),
                    in_=scores[g][h][:].rearrange("p (a r) -> p r a", a=PACK),
                    func=ACT.Exp,
                    bias=neg_max[g][:, 0:1],
                    scale=1.0,
                    accum_out=bank_sums[:, h : h + 1],
                )
            probs[g] = row_tile
            sums[g] = bank_sums

        def add_sums(g):
            total = rows_pool.tile([P, 1], F32, tag="row_sum")
            nc.vector.tensor_reduce(out=total[:], in_=sums[g][:], axis=AXIS.X, op=ALU.add)
            row_sum[g] = total

        def invert_sum(g):
            inverse = rows_pool.tile([P, 1], F32, tag="inv_sum")
            nc.vector.reciprocal(out=inverse[:], in_=row_sum[g][:])
            inv_sum[g] = inverse

        def store(g, cols):
            nc.sync.dma_start(out=out_rows_dram[g * P : (g + 1) * P, cols], in_=probs[g][:, cols])

        def scale_on_gpsimd(g):
            nc.gpsimd.tensor_scalar(
                out=probs[g][:], in0=probs[g][:], scalar1=inv_sum[g][:, 0:1], scalar2=0.0,
                op0=ALU.mult, op1=ALU.add,
            )
            store(g, slice(0, TOKENS))

        def scale_on_vector(g, cols):
            nc.vector.tensor_scalar_mul(out=probs[g][:, cols], in0=probs[g][:, cols], scalar1=inv_sum[g][:, 0:1])
            store(g, cols)

        def scale_on_scalar(g, cols):
            nc.scalar.activation(
                out=probs[g][:, cols], in_=probs[g][:, cols], func=ACT.Copy, scale=inv_sum[g][:, 0:1]
            )
            store(g, cols)

        on_scalar = nc.scalar.copy
        on_vector = nc.vector.tensor_copy

        with tc.manual_schedule():
            keep_busy(4)
            flip("wq", wq_rows, 0)
            flip("wq", wq_rows, 1)
            keep_busy(2)
            unflip(on_vector, "wq", 0)
            unflip(on_scalar, "wq", 1)
            interleave_x(on_vector, 0)
            interleave_x(on_scalar, 1)
            quantise_rows("wq", 0)
            quantise_rows("wq", 1)
            quantise_chunk("x", 0)
            quantise_chunk("x", 1)
            flip("k0", k_rows[0], 0)
            flip("k0", k_rows[0], 1)
            project_tile(0)
            project_tile(1)
            unflip(on_scalar, "k0", 0)
            unflip(on_scalar, "k0", 1)
            interleave_x(on_vector, 2)
            interleave_x(on_scalar, 3)
            mix_tile(0)
            mix_tile(1)
            project_chunk(1)
            for pair in range(2):
                flip("k1", k_rows[1], pair)
                unflip(on_scalar, "k1", pair)
            quantise_chunk("x", 2)
            quantise_rows("k0", 0)
            quantise_rows("k0", 1)
            quantise_chunk("q", 0)
            quantise_chunk("x", 3)
            quantise_rows("k1", 0)
            quantise_rows("k1", 1)
            project_chunk(2)
            score(0)
            project_chunk(3)
            score(1)
            for c in range(1, CHUNKS):
                empty_chunk(c, 0)
                empty_chunk(c, 1)
            mix_chunk(on_vector, 1)
            bank_maximum(0, 0)
            bank_maximum(0, 1)
            quantise_chunk("q", 1)
            negate_maximum(0)
            exponentials(0)
            mix_chunk(on_scalar, 3)
            bank_maximum(1, 0)
            mix_chunk(on_vector, 2)
            bank_maximum(1, 1)
            quantise_chunk("q", 2)
            negate_maximum(1)
            exponentials(1)
            score(2)
            add_sums(0)
            bank_maximum(2, 0)
            quantise_chunk("q", 3)
            invert_sum(0)
            scale_on_gpsimd(0)
            bank_maximum(2, 1)
            score(3)
            for g in range(3, TILES):
                negate_maximum(g - 1)
                exponentials(g - 1)
                bank_maximum(g, 0)
                add_sums(g - 2)
                bank_maximum(g, 1)
                invert_sum(g - 2)
                if g - 2 < GPSIMD_TILES:
                    scale_on_gpsimd(g - 2)
                if g + 1 < TILES:
                    score(g + 1)
            negate_maximum(TILES - 1)
            exponentials(TILES - 1)
            for g in range(GPSIMD_TILES, TILES):
                if g > TILES - 3:
                    add_sums(g)
                    invert_sum(g)
                if g == TILES - 1:
                    scale_on_vector(g, slice(0, VECTOR_COLUMNS))
                    scale_on_scalar(g, slice(VECTOR_COLUMNS, TOKENS))
                else:
                    scale_on_vector(g, half(0))
                    scale_on_vector(g, half(1))
